import numpy as np
import ml_dtypes


def mxq(x, axis, fmt="e4m3"):
    dtype, down = {"e4m3": (ml_dtypes.float8_e4m3fn, 7), "e5m2": (ml_dtypes.float8_e5m2, 14)}[fmt]
    v = np.moveaxis(np.asarray(x, np.float32).astype(ml_dtypes.bfloat16).astype(np.float64), axis, -1)
    blocks = v.reshape(v.shape[:-1] + (-1, 32))
    amax = np.abs(blocks).max(-1, keepdims=True)
    byte = np.maximum(np.where(amax > 0, np.frexp(amax)[1] - 1 + 127, 0) - down, 1)
    scale = np.exp2(byte - 127.0)
    codes = (blocks / scale).astype(np.float32).astype(dtype).astype(np.float64)
    return np.moveaxis((codes * scale).reshape(v.shape), -1, axis)


WIDE = False


def mx_kscale(k, group=512):
    if not WIDE:
        return np.ones(k)
    levels = np.array([10, -10, 5, -5, 0])
    if group != 512:
        return np.exp2(np.random.permutation(np.resize(levels, k // group))).repeat(group)
    a = np.random.permutation(np.resize(levels, k // 512 * 4)).reshape(k // 512, 4)
    idx = np.arange(k)
    return np.exp2(a[idx // 512, idx % 128 // 32])


BF16 = ml_dtypes.bfloat16


def bf(x):
    return np.asarray(x, np.float32).astype(BF16)


def f64(x):
    return np.asarray(x).astype(np.float64)


B, T, D, F = 2, 8, 4096, 1024
TRIPLES = [(1, 2, 3), (1, 4, 5), (1, 7, 6), (2, 4, 6), (2, 5, 7), (3, 4, 7), (3, 6, 5)]
O = len(TRIPLES) + 1
D8, F8 = D // O, F // O


def oct_table():
    tab = [[None] * O for _ in range(O)]
    tab[0][0] = (0, 1.0)
    for i in range(1, O):
        tab[i][i] = (0, 1.0)
        tab[0][i] = (i, 1.0)
        tab[i][0] = (i, -1.0)
    for a, b, c in TRIPLES:
        for p, q, r in ((a, b, c), (b, c, a), (c, a, b)):
            tab[q][r] = (p, 1.0)
            tab[p][r] = (q, -1.0)
    return tab


def oct_linear(xq, w):
    tab = oct_table()
    p = (xq @ mxq(w.reshape(F, D8).T, 0, "e4m3")).reshape(B, T, O, O, F8)
    return np.concatenate([sum(tab[i][k][1] * p[:, :, i, tab[i][k][0]] for i in range(O)) for k in range(O)], axis=2)


def silu(v):
    return v / (1.0 + np.exp(-v))


def setup_inputs():
    s8 = mx_kscale(D8, D8 // 2)
    return {"x": bf(np.random.standard_normal((B, T, D)) * np.tile(s8, O)),
            "wq_gate": bf(np.random.standard_normal((O, F8, D8)) / np.sqrt(D) / s8),
            "wq_up": bf(np.random.standard_normal((O, F8, D8)) / np.sqrt(D) / s8)}


def reference(x, wq_gate, wq_up):
    xq = mxq(f64(x).reshape(B, T, O, D8), 3, "e4m3")
    gate = oct_linear(xq, f64(wq_gate))
    up = oct_linear(xq, f64(wq_up))
    return silu(gate) * up

@@ -1,0 +1,182 @@
+from contextlib import ExitStack
+
+import concourse.mybir as mybir
+from concourse.masks import make_identity
+
+BF16 = mybir.dt.bfloat16
+F32 = mybir.dt.float32
+U32 = mybir.dt.uint32
+U8 = mybir.dt.uint8
+FP8X4 = mybir.dt.float8_e4m3fn_x4
+MULT = mybir.AluOpType.mult
+SILU = mybir.ActivationFunctionType.Silu
+
+P = 128
+PACK = 4
+UNITS = 8
+TOKENS = 16
+D8 = 512
+F8 = 128
+HALVES = 2
+WORDS = D8 // 2
+COLS = TOKENS * UNITS
+PAIR = 2 * F8
+UNITS_PER_ROUND = 2
+ROUNDS = UNITS // UNITS_PER_ROUND
+TRIPLES = ((1, 2, 3), (1, 4, 5), (1, 7, 6), (2, 4, 6), (2, 5, 7), (3, 4, 7), (3, 6, 5))
+
+FLOPS = 2 * 2 * TOKENS * UNITS * UNITS * F8 * D8
+
+
+def unit_product_sign(a, b):
+    if a == 0 or b == 0:
+        return 1.0
+    if a == b:
+        return -1.0
+    for triple in TRIPLES:
+        for turn in range(3):
+            first, second = triple[turn], triple[(turn + 1) % 3]
+            if (a, b) == (first, second):
+                return 1.0
+            if (a, b) == (second, first):
+                return -1.0
+    raise ValueError("not a pair of octonion units")
+
+
+def variant_sign(j, k):
+    return unit_product_sign(j, j ^ k)
+
+
+def top_bit(j):
+    return max(bit for bit in (1, 2, 4) if bit <= j)
+
+
+def runs_of_minus(signs):
+    runs = []
+    for place, sign in enumerate(signs):
+        if sign < 0 and runs and runs[-1][1] == place:
+            runs[-1] = (runs[-1][0], place + 1)
+        elif sign < 0:
+            runs.append((place, place + 1))
+    return runs
+
+
+def tile_swiglumlp_pa_s_kernel(tc, x, wq_gate, wq_up, out):
+    nc = tc.nc
+    with ExitStack() as stack:
+        keep = stack.enter_context(tc.tile_pool(name="keep", bufs=1))
+        rows = stack.enter_context(tc.tile_pool(name="rows", bufs=ROUNDS))
+        psum_keep = stack.enter_context(tc.psum_pool(name="psum_keep", bufs=1))
+        psum_w = stack.enter_context(tc.psum_pool(name="psum_w", bufs=2 * UNITS_PER_ROUND))
+
+        x_rows = keep.tile([P, D8], BF16)
+        nc.sync.dma_start(out=x_rows[:], in_=x.rearrange("b t (i d) -> (b t i) d", i=UNITS))
+        loaded = []
+        for r in range(ROUNDS):
+            units = slice(r * UNITS_PER_ROUND, (r + 1) * UNITS_PER_ROUND)
+            gate_rows = rows.tile([P, UNITS_PER_ROUND, D8], BF16)
+            nc.sync.dma_start(out=gate_rows[:], in_=wq_gate[units].rearrange("j o d -> o j d"))
+            up_rows = rows.tile([P, UNITS_PER_ROUND, D8], BF16)
+            nc.sync.dma_start(out=up_rows[:], in_=wq_up[units].rearrange("j o d -> o j d"))
+            loaded.append((gate_rows, up_rows))
+
+        warm = keep.tile([P, 1], F32)
+        nc.vector.memset(warm[:], 0.0)
+        nc.scalar.activation(out=warm[:], in_=warm[:], func=SILU)
+
+        identity = keep.tile([P, P], F32)
+        make_identity(nc, identity[:])
+
+        ratio = keep.tile([P, UNITS * UNITS * PACK], BF16)
+        nc.vector.memset(ratio[:], 1.0)
+        for j in range(1, UNITS):
+            b = top_bit(j)
+            signs = [variant_sign(j, k) * variant_sign(j - b, k ^ b) for k in range(UNITS)]
+            for start, stop in runs_of_minus(signs):
+                nc.vector.memset(ratio[:, (j * UNITS + start) * PACK : (j * UNITS + stop) * PACK], -1.0)
+
+        variants = keep.tile([P, UNITS * COLS * PACK], BF16, align_bytes=64)
+        x_codes = keep.tile([P, UNITS * COLS], U32, align_bytes=64)
+        x_scales = keep.tile([P, UNITS * COLS], U8, align_bytes=64)
+
+        x_t = psum_keep.tile([P, HALVES, COLS], F32)
+        for u in range(HALVES):
+            nc.tensor.transpose(x_t[:, u, :], x_rows[:].bitcast(F32)[:, u:WORDS:HALVES], identity[:])
+        nc.scalar.copy(
+            out=variants[:, 0 : COLS * PACK].bitcast(F32).rearrange("p (c u) -> p c u", u=HALVES),
+            in_=x_t[:].rearrange("p u c -> p c u"),
+        )
+
+        def make_variant(j):
+            b = top_bit(j)
+            split = "p (n a h c) -> p n a h c"
+            new = variants[:, j * COLS * PACK : (j + 1) * COLS * PACK].rearrange(split, n=TOKENS, h=2, c=b * PACK)
+            old = variants[:, (j - b) * COLS * PACK : (j - b + 1) * COLS * PACK].rearrange(split, n=TOKENS, h=2, c=b * PACK)
+            factor = ratio[:, j * UNITS * PACK : (j + 1) * UNITS * PACK].rearrange("p (a h c) -> p a h c", h=2, c=b * PACK)
+            for h in range(2):
+                nc.vector.tensor_tensor(
+                    out=new[:, :, :, h, :],
+                    in0=old[:, :, :, 1 - h, :],
+                    in1=factor[:, :, h, :].unsqueeze(1).to_broadcast([P, TOKENS, UNITS // (2 * b), b * PACK]),
+                    op=MULT,
+                )
+
+        def quantise_variants(first, count):
+            nc.vector.quantize_mx(
+                out=x_codes[:, first * COLS : (first + count) * COLS].bitcast(FP8X4),
+                scales=x_scales[:, first * COLS : (first + count) * COLS],
+                in_=variants[:, first * COLS * PACK : (first + count) * COLS * PACK],
+            )
+
+        for j in range(1, UNITS):
+            make_variant(j)
+        quantise_variants(0, UNITS // 2)
+        quantise_variants(UNITS // 2, UNITS // 2)
+
+        w_grouped = keep.tile([P, UNITS * PAIR * PACK], BF16, align_bytes=64)
+        w_codes = keep.tile([P, UNITS * PAIR], U32, align_bytes=64)
+        w_scales = keep.tile([P, UNITS * PAIR], U8, align_bytes=64)
+        gate_up = psum_keep.tile([P, PAIR], F32)
+
+        def prepare_weights(r):
+            banks = []
+            for jj in range(UNITS_PER_ROUND):
+                w_t = psum_w.tile([P, HALVES, PAIR], F32)
+                banks.append(w_t)
+            for m in range(2):
+                for jj in range(UNITS_PER_ROUND):
+                    words = loaded[r][m][:, jj, :].bitcast(F32)
+                    for u in range(HALVES):
+                        nc.tensor.transpose(banks[jj][:, u, m * F8 : (m + 1) * F8], words[:, u:WORDS:HALVES], identity[:])
+            for jj in range(UNITS_PER_ROUND):
+                j = r * UNITS_PER_ROUND + jj
+                nc.scalar.copy(
+                    out=w_grouped[:, j * PAIR * PACK : (j + 1) * PAIR * PACK]
+                    .bitcast(F32)
+                    .rearrange("p (c u) -> p c u", u=HALVES),
+                    in_=banks[jj][:].rearrange("p u c -> p c u"),
+                )
+                nc.vector.quantize_mx(
+                    out=w_codes[:, j * PAIR : (j + 1) * PAIR].bitcast(FP8X4),
+                    scales=w_scales[:, j * PAIR : (j + 1) * PAIR],
+                    in_=w_grouped[:, j * PAIR * PACK : (j + 1) * PAIR * PACK],
+                )
+
+        for r in range(ROUNDS):
+            prepare_weights(r)
+        for j in range(UNITS):
+            nc.tensor.matmul_mx(
+                out=gate_up[:],
+                lhsT=x_codes[:, j * COLS : (j + 1) * COLS].bitcast(FP8X4),
+                lhsT_scale=x_scales[:, j * COLS : (j + 1) * COLS],
+                rhs=w_codes[:, j * PAIR : (j + 1) * PAIR].bitcast(FP8X4),
+                rhs_scale=w_scales[:, j * PAIR : (j + 1) * PAIR],
+                start=(j == 0),
+                stop=(j == UNITS - 1),
+            )
+
+        gate_silu = keep.tile([P, F8], F32)
+        nc.scalar.activation(out=gate_silu[:], in_=gate_up[:, 0:F8], func=SILU)
+        result = keep.tile([P, F8], F32)
+        nc.vector.tensor_tensor(out=result[:], in0=gate_silu[:], in1=gate_up[:, F8:PAIR], op=MULT)
+        nc.sync.dma_start(out=out.rearrange("b t (k o) -> (b t k) o", k=UNITS), in_=result[:])

@@ -21,8 +21,9 @@ HALVES = 2
 WORDS = D8 // 2
 COLS = TOKENS * UNITS
 PAIR = 2 * F8
-UNITS_PER_ROUND = 2
-ROUNDS = UNITS // UNITS_PER_ROUND
+UNITS_PER_LOAD = 2
+SINGLE_UNITS = 2
+W_BANKS = 6
 TRIPLES = ((1, 2, 3), (1, 4, 5), (1, 7, 6), (2, 4, 6), (2, 5, 7), (3, 4, 7), (3, 6, 5))
 
 FLOPS = 2 * 2 * TOKENS * UNITS * UNITS * F8 * D8
@@ -53,11 +54,11 @@ def top_bit(j):
 
 def runs_of_minus(signs):
     runs = []
-    for place, sign in enumerate(signs):
-        if sign < 0 and runs and runs[-1][1] == place:
-            runs[-1] = (runs[-1][0], place + 1)
+    for k, sign in enumerate(signs):
+        if sign < 0 and runs and runs[-1][1] == k:
+            runs[-1] = (runs[-1][0], k + 1)
         elif sign < 0:
-            runs.append((place, place + 1))
+            runs.append((k, k + 1))
     return runs
 
 
@@ -65,20 +66,20 @@ def tile_swiglumlp_pa_s_kernel(tc, x, wq_gate, wq_up, out):
     nc = tc.nc
     with ExitStack() as stack:
         keep = stack.enter_context(tc.tile_pool(name="keep", bufs=1))
-        rows = stack.enter_context(tc.tile_pool(name="rows", bufs=ROUNDS))
         psum_keep = stack.enter_context(tc.psum_pool(name="psum_keep", bufs=1))
-        psum_w = stack.enter_context(tc.psum_pool(name="psum_w", bufs=2 * UNITS_PER_ROUND))
+        psum_w = stack.enter_context(tc.psum_pool(name="psum_w", bufs=W_BANKS))
 
         x_rows = keep.tile([P, D8], BF16)
         nc.sync.dma_start(out=x_rows[:], in_=x.rearrange("b t (i d) -> (b t i) d", i=UNITS))
-        loaded = []
-        for r in range(ROUNDS):
-            units = slice(r * UNITS_PER_ROUND, (r + 1) * UNITS_PER_ROUND)
-            gate_rows = rows.tile([P, UNITS_PER_ROUND, D8], BF16)
-            nc.sync.dma_start(out=gate_rows[:], in_=wq_gate[units].rearrange("j o d -> o j d"))
-            up_rows = rows.tile([P, UNITS_PER_ROUND, D8], BF16)
-            nc.sync.dma_start(out=up_rows[:], in_=wq_up[units].rearrange("j o d -> o j d"))
-            loaded.append((gate_rows, up_rows))
+        spans = [(first, UNITS_PER_LOAD) for first in range(0, UNITS - SINGLE_UNITS, UNITS_PER_LOAD)]
+        spans += [(first, 1) for first in range(UNITS - SINGLE_UNITS, UNITS)]
+        rows = stack.enter_context(tc.tile_pool(name="rows", bufs=2 * len(spans)))
+        matrices = []
+        for first, count in spans:
+            for m, weight in enumerate((wq_gate, wq_up)):
+                w_rows = rows.tile([P, count, D8], BF16)
+                nc.sync.dma_start(out=w_rows[:], in_=weight[first : first + count].rearrange("j o d -> o j d"))
+                matrices += [(first + jj, m, w_rows[:, jj, :]) for jj in range(count)]
 
         warm = keep.tile([P, 1], F32)
         nc.vector.memset(warm[:], 0.0)
@@ -138,32 +139,20 @@ def tile_swiglumlp_pa_s_kernel(tc, x, wq_gate, wq_up, out):
         w_scales = keep.tile([P, UNITS * PAIR], U8, align_bytes=64)
         gate_up = psum_keep.tile([P, PAIR], F32)
 
-        def prepare_weights(r):
-            banks = []
-            for jj in range(UNITS_PER_ROUND):
-                w_t = psum_w.tile([P, HALVES, PAIR], F32)
-                banks.append(w_t)
-            for m in range(2):
-                for jj in range(UNITS_PER_ROUND):
-                    words = loaded[r][m][:, jj, :].bitcast(F32)
-                    for u in range(HALVES):
-                        nc.tensor.transpose(banks[jj][:, u, m * F8 : (m + 1) * F8], words[:, u:WORDS:HALVES], identity[:])
-            for jj in range(UNITS_PER_ROUND):
-                j = r * UNITS_PER_ROUND + jj
-                nc.scalar.copy(
-                    out=w_grouped[:, j * PAIR * PACK : (j + 1) * PAIR * PACK]
-                    .bitcast(F32)
-                    .rearrange("p (c u) -> p c u", u=HALVES),
-                    in_=banks[jj][:].rearrange("p u c -> p c u"),
-                )
-                nc.vector.quantize_mx(
-                    out=w_codes[:, j * PAIR : (j + 1) * PAIR].bitcast(FP8X4),
-                    scales=w_scales[:, j * PAIR : (j + 1) * PAIR],
-                    in_=w_grouped[:, j * PAIR * PACK : (j + 1) * PAIR * PACK],
-                )
-
-        for r in range(ROUNDS):
-            prepare_weights(r)
+        for j, m, w_matrix in matrices:
+            w_t = psum_w.tile([P, HALVES, F8], F32)
+            for u in range(HALVES):
+                nc.tensor.transpose(w_t[:, u, :], w_matrix.bitcast(F32)[:, u:WORDS:HALVES], identity[:])
+            place = j * PAIR + m * F8
+            nc.scalar.copy(
+                out=w_grouped[:, place * PACK : (place + F8) * PACK].bitcast(F32).rearrange("p (c u) -> p c u", u=HALVES),
+                in_=w_t[:].rearrange("p u c -> p c u"),
+            )
+            nc.vector.quantize_mx(
+                out=w_codes[:, place : place + F8].bitcast(FP8X4),
+                scales=w_scales[:, place : place + F8],
+                in_=w_grouped[:, place * PACK : (place + F8) * PACK],
+            )
         for j in range(UNITS):
             nc.tensor.matmul_mx(
                 out=gate_up[:],

@@ -88,13 +88,14 @@ def tile_swiglumlp_pa_s_kernel(tc, x, wq_gate, wq_up, out):
         identity = keep.tile([P, P], F32)
         make_identity(nc, identity[:])
 
-        ratio = keep.tile([P, UNITS * UNITS * PACK], BF16)
+        ratio = keep.tile([P, UNITS * COLS * PACK], BF16)
         nc.vector.memset(ratio[:], 1.0)
+        ratio_by_token = ratio[:].rearrange("p (j n c) -> p j n c", j=UNITS, n=TOKENS)
         for j in range(1, UNITS):
             b = top_bit(j)
             signs = [variant_sign(j, k) * variant_sign(j - b, k ^ b) for k in range(UNITS)]
             for start, stop in runs_of_minus(signs):
-                nc.vector.memset(ratio[:, (j * UNITS + start) * PACK : (j * UNITS + stop) * PACK], -1.0)
+                nc.vector.memset(ratio_by_token[:, j, :, start * PACK : stop * PACK], -1.0)
 
         variants = keep.tile([P, UNITS * COLS * PACK], BF16, align_bytes=64)
         x_codes = keep.tile([P, UNITS * COLS], U32, align_bytes=64)
@@ -108,19 +109,13 @@ def tile_swiglumlp_pa_s_kernel(tc, x, wq_gate, wq_up, out):
             in_=x_t[:].rearrange("p u c -> p c u"),
         )
 
-        def make_variant(j):
-            b = top_bit(j)
-            split = "p (n a h c) -> p n a h c"
-            new = variants[:, j * COLS * PACK : (j + 1) * COLS * PACK].rearrange(split, n=TOKENS, h=2, c=b * PACK)
-            old = variants[:, (j - b) * COLS * PACK : (j - b + 1) * COLS * PACK].rearrange(split, n=TOKENS, h=2, c=b * PACK)
-            factor = ratio[:, j * UNITS * PACK : (j + 1) * UNITS * PACK].rearrange("p (a h c) -> p a h c", h=2, c=b * PACK)
+        def make_variants(b):
+            split = "p (j g h c) -> p j g h c"
+            new = variants[:, b * COLS * PACK : 2 * b * COLS * PACK].rearrange(split, j=b, h=2, c=b * PACK)
+            old = variants[:, 0 : b * COLS * PACK].rearrange(split, j=b, h=2, c=b * PACK)
+            factor = ratio[:, b * COLS * PACK : 2 * b * COLS * PACK].rearrange(split, j=b, h=2, c=b * PACK)
             for h in range(2):
-                nc.vector.tensor_tensor(
-                    out=new[:, :, :, h, :],
-                    in0=old[:, :, :, 1 - h, :],
-                    in1=factor[:, :, h, :].unsqueeze(1).to_broadcast([P, TOKENS, UNITS // (2 * b), b * PACK]),
-                    op=MULT,
-                )
+                nc.vector.tensor_tensor(out=new[:, :, :, h, :], in0=old[:, :, :, 1 - h, :], in1=factor[:, :, :, h, :], op=MULT)
 
         def quantise_variants(first, count):
             nc.vector.quantize_mx(
@@ -129,8 +124,8 @@ def tile_swiglumlp_pa_s_kernel(tc, x, wq_gate, wq_up, out):
                 in_=variants[:, first * COLS * PACK : (first + count) * COLS * PACK],
             )
 
-        for j in range(1, UNITS):
-            make_variant(j)
+        for b in (1, 2, 4):
+            make_variants(b)
         quantise_variants(0, UNITS // 2)
         quantise_variants(UNITS // 2, UNITS // 2)
 

@@ -48,20 +48,6 @@ def variant_sign(j, k):
     return unit_product_sign(j, j ^ k)
 
 
-def top_bit(j):
-    return max(bit for bit in (1, 2, 4) if bit <= j)
-
-
-def runs_of_minus(signs):
-    runs = []
-    for k, sign in enumerate(signs):
-        if sign < 0 and runs and runs[-1][1] == k:
-            runs[-1] = (runs[-1][0], k + 1)
-        elif sign < 0:
-            runs.append((k, k + 1))
-    return runs
-
-
 def tile_swiglumlp_pa_s_kernel(tc, x, wq_gate, wq_up, out):
     nc = tc.nc
     with ExitStack() as stack:
@@ -88,15 +74,6 @@ def tile_swiglumlp_pa_s_kernel(tc, x, wq_gate, wq_up, out):
         identity = keep.tile([P, P], F32)
         make_identity(nc, identity[:])
 
-        ratio = keep.tile([P, UNITS * COLS * PACK], BF16)
-        nc.vector.memset(ratio[:], 1.0)
-        ratio_by_token = ratio[:].rearrange("p (j n c) -> p j n c", j=UNITS, n=TOKENS)
-        for j in range(1, UNITS):
-            b = top_bit(j)
-            signs = [variant_sign(j, k) * variant_sign(j - b, k ^ b) for k in range(UNITS)]
-            for start, stop in runs_of_minus(signs):
-                nc.vector.memset(ratio_by_token[:, j, :, start * PACK : stop * PACK], -1.0)
-
         variants = keep.tile([P, UNITS * COLS * PACK], BF16, align_bytes=64)
         x_codes = keep.tile([P, UNITS * COLS], U32, align_bytes=64)
         x_scales = keep.tile([P, UNITS * COLS], U8, align_bytes=64)
@@ -109,13 +86,28 @@ def tile_swiglumlp_pa_s_kernel(tc, x, wq_gate, wq_up, out):
             in_=x_t[:].rearrange("p u c -> p c u"),
         )
 
+        def times_sign(out, in_, sign):
+            if sign > 0:
+                nc.vector.tensor_copy(out=out, in_=in_)
+            else:
+                nc.vector.tensor_scalar(out=out, in0=in_, scalar1=-1.0, scalar2=None, op0=MULT)
+
         def make_variants(b):
+            ratio = [[variant_sign(j, k) * variant_sign(j - b, k ^ b) for k in range(UNITS)] for j in range(b, 2 * b)]
             split = "p (j g h c) -> p j g h c"
             new = variants[:, b * COLS * PACK : 2 * b * COLS * PACK].rearrange(split, j=b, h=2, c=b * PACK)
             old = variants[:, 0 : b * COLS * PACK].rearrange(split, j=b, h=2, c=b * PACK)
-            factor = ratio[:, b * COLS * PACK : 2 * b * COLS * PACK].rearrange(split, j=b, h=2, c=b * PACK)
+            common = []
             for h in range(2):
-                nc.vector.tensor_tensor(out=new[:, :, :, h, :], in0=old[:, :, :, 1 - h, :], in1=factor[:, :, :, h, :], op=MULT)
+                total = sum(row[k] for row in ratio for k in range(UNITS) if bool(k & b) == bool(h))
+                common.append(1.0 if total > 0 else -1.0)
+                times_sign(new[:, :, :, h, :], old[:, :, :, 1 - h, :], common[h])
+            for j in range(b, 2 * b):
+                others = [k for k in range(UNITS) if ratio[j - b][k] != common[1 if k & b else 0]]
+                assert len(others) == 2
+                by_token = variants[:, j * COLS * PACK : (j + 1) * COLS * PACK].rearrange("p (n k t) -> p n k t", k=UNITS, t=PACK)
+                cells = by_token[:, :, others[0] : others[1] + 1 : others[1] - others[0], :]
+                times_sign(cells, cells, -1.0)
 
         def quantise_variants(first, count):
             nc.vector.quantize_mx(

from contextlib import ExitStack

import concourse.mybir as mybir
from concourse.masks import make_identity

BF16 = mybir.dt.bfloat16
F32 = mybir.dt.float32
U32 = mybir.dt.uint32
U8 = mybir.dt.uint8
FP8X4 = mybir.dt.float8_e4m3fn_x4
MULT = mybir.AluOpType.mult
SILU = mybir.ActivationFunctionType.Silu

P = 128
PACK = 4
UNITS = 8
TOKENS = 16
D8 = 512
F8 = 128
HALVES = 2
WORDS = D8 // 2
COLS = TOKENS * UNITS
PAIR = 2 * F8
UNITS_PER_LOAD = 2
SINGLE_UNITS = 2
W_BANKS = 6
TRIPLES = ((1, 2, 3), (1, 4, 5), (1, 7, 6), (2, 4, 6), (2, 5, 7), (3, 4, 7), (3, 6, 5))

FLOPS = 2 * 2 * TOKENS * UNITS * UNITS * F8 * D8


def unit_product_sign(a, b):
    if a == 0 or b == 0:
        return 1.0
    if a == b:
        return -1.0
    for triple in TRIPLES:
        for turn in range(3):
            first, second = triple[turn], triple[(turn + 1) % 3]
            if (a, b) == (first, second):
                return 1.0
            if (a, b) == (second, first):
                return -1.0
    raise ValueError("not a pair of octonion units")


def variant_sign(j, k):
    return unit_product_sign(j, j ^ k)


def tile_swiglumlp_pa_s_kernel(tc, x, wq_gate, wq_up, out):
    nc = tc.nc
    with ExitStack() as stack:
        keep = stack.enter_context(tc.tile_pool(name="keep", bufs=1))
        psum_keep = stack.enter_context(tc.psum_pool(name="psum_keep", bufs=1))
        psum_w = stack.enter_context(tc.psum_pool(name="psum_w", bufs=W_BANKS))

        x_rows = keep.tile([P, D8], BF16)
        nc.sync.dma_start(out=x_rows[:], in_=x.rearrange("b t (i d) -> (b t i) d", i=UNITS))
        spans = [(first, UNITS_PER_LOAD) for first in range(0, UNITS - SINGLE_UNITS, UNITS_PER_LOAD)]
        spans += [(first, 1) for first in range(UNITS - SINGLE_UNITS, UNITS)]
        rows = stack.enter_context(tc.tile_pool(name="rows", bufs=2 * len(spans)))
        matrices = []
        for first, count in spans:
            for m, weight in enumerate((wq_gate, wq_up)):
                w_rows = rows.tile([P, count, D8], BF16)
                nc.sync.dma_start(out=w_rows[:], in_=weight[first : first + count].rearrange("j o d -> o j d"))
                matrices += [(first + jj, m, w_rows[:, jj, :]) for jj in range(count)]

        warm = keep.tile([P, 1], F32)
        nc.vector.memset(warm[:], 0.0)
        nc.scalar.activation(out=warm[:], in_=warm[:], func=SILU)

        identity = keep.tile([P, P], F32)
        make_identity(nc, identity[:])

        variants = keep.tile([P, UNITS * COLS * PACK], BF16, align_bytes=64)
        x_codes = keep.tile([P, UNITS * COLS], U32, align_bytes=64)
        x_scales = keep.tile([P, UNITS * COLS], U8, align_bytes=64)

        x_t = psum_keep.tile([P, HALVES, COLS], F32)
        for u in range(HALVES):
            nc.tensor.transpose(x_t[:, u, :], x_rows[:].bitcast(F32)[:, u:WORDS:HALVES], identity[:])
        nc.scalar.copy(
            out=variants[:, 0 : COLS * PACK].bitcast(F32).rearrange("p (c u) -> p c u", u=HALVES),
            in_=x_t[:].rearrange("p u c -> p c u"),
        )

        def times_sign(out, in_, sign):
            if sign > 0:
                nc.vector.tensor_copy(out=out, in_=in_)
            else:
                nc.vector.tensor_scalar(out=out, in0=in_, scalar1=-1.0, scalar2=None, op0=MULT)

        def make_variants(b):
            ratio = [[variant_sign(j, k) * variant_sign(j - b, k ^ b) for k in range(UNITS)] for j in range(b, 2 * b)]
            split = "p (j g h c) -> p j g h c"
            new = variants[:, b * COLS * PACK : 2 * b * COLS * PACK].rearrange(split, j=b, h=2, c=b * PACK)
            old = variants[:, 0 : b * COLS * PACK].rearrange(split, j=b, h=2, c=b * PACK)
            common = []
            for h in range(2):
                total = sum(row[k] for row in ratio for k in range(UNITS) if bool(k & b) == bool(h))
                common.append(1.0 if total > 0 else -1.0)
                times_sign(new[:, :, :, h, :], old[:, :, :, 1 - h, :], common[h])
            for j in range(b, 2 * b):
                others = [k for k in range(UNITS) if ratio[j - b][k] != common[1 if k & b else 0]]
                assert len(others) == 2
                by_token = variants[:, j * COLS * PACK : (j + 1) * COLS * PACK].rearrange("p (n k t) -> p n k t", k=UNITS, t=PACK)
                cells = by_token[:, :, others[0] : others[1] + 1 : others[1] - others[0], :]
                times_sign(cells, cells, -1.0)

        def quantise_variants(first, count):
            nc.vector.quantize_mx(
                out=x_codes[:, first * COLS : (first + count) * COLS].bitcast(FP8X4),
                scales=x_scales[:, first * COLS : (first + count) * COLS],
                in_=variants[:, first * COLS * PACK : (first + count) * COLS * PACK],
            )

        for b in (1, 2, 4):
            make_variants(b)
        quantise_variants(0, UNITS // 2)
        quantise_variants(UNITS // 2, UNITS // 2)

        w_grouped = keep.tile([P, UNITS * PAIR * PACK], BF16, align_bytes=64)
        w_codes = keep.tile([P, UNITS * PAIR], U32, align_bytes=64)
        w_scales = keep.tile([P, UNITS * PAIR], U8, align_bytes=64)
        gate_up = psum_keep.tile([P, PAIR], F32)

        for j, m, w_matrix in matrices:
            w_t = psum_w.tile([P, HALVES, F8], F32)
            for u in range(HALVES):
                nc.tensor.transpose(w_t[:, u, :], w_matrix.bitcast(F32)[:, u:WORDS:HALVES], identity[:])
            place = j * PAIR + m * F8
            nc.scalar.copy(
                out=w_grouped[:, place * PACK : (place + F8) * PACK].bitcast(F32).rearrange("p (c u) -> p c u", u=HALVES),
                in_=w_t[:].rearrange("p u c -> p c u"),
            )
            nc.vector.quantize_mx(
                out=w_codes[:, place : place + F8].bitcast(FP8X4),
                scales=w_scales[:, place : place + F8],
                in_=w_grouped[:, place * PACK : (place + F8) * PACK],
            )
        for j in range(UNITS):
            nc.tensor.matmul_mx(
                out=gate_up[:],
                lhsT=x_codes[:, j * COLS : (j + 1) * COLS].bitcast(FP8X4),
                lhsT_scale=x_scales[:, j * COLS : (j + 1) * COLS],
                rhs=w_codes[:, j * PAIR : (j + 1) * PAIR].bitcast(FP8X4),
                rhs_scale=w_scales[:, j * PAIR : (j + 1) * PAIR],
                start=(j == 0),
                stop=(j == UNITS - 1),
            )

        gate_silu = keep.tile([P, F8], F32)
        nc.scalar.activation(out=gate_silu[:], in_=gate_up[:, 0:F8], func=SILU)
        result = keep.tile([P, F8], F32)
        nc.vector.tensor_tensor(out=result[:], in0=gate_silu[:], in1=gate_up[:, F8:PAIR], op=MULT)
        nc.sync.dma_start(out=out.rearrange("b t (k o) -> (b t k) o", k=UNITS), in_=result[:])
